import numpy as np
import ml_dtypes


def mxq(x, axis, fmt="e4m3"):
    dtype, down = {"e4m3": (ml_dtypes.float8_e4m3fn, 7), "e5m2": (ml_dtypes.float8_e5m2, 14)}[fmt]
    v = np.moveaxis(np.asarray(x, np.float32).astype(ml_dtypes.bfloat16).astype(np.float64), axis, -1)
    blocks = v.reshape(v.shape[:-1] + (-1, 32))
    amax = np.abs(blocks).max(-1, keepdims=True)
    byte = np.maximum(np.where(amax > 0, np.frexp(amax)[1] - 1 + 127, 0) - down, 1)
    scale = np.exp2(byte - 127.0)
    codes = (blocks / scale).astype(np.float32).astype(dtype).astype(np.float64)
    return np.moveaxis((codes * scale).reshape(v.shape), -1, axis)


WIDE = False


def mx_kscale(k):
    if not WIDE:
        return np.ones(k)
    levels = np.array([10, -10, 5, -5, 0])
    a = np.random.permutation(np.resize(levels, k // 512 * 4)).reshape(k // 512, 4)
    idx = np.arange(k)
    return np.exp2(a[idx // 512, idx % 128 // 32])


BF16 = ml_dtypes.bfloat16


def bf(x):
    return np.asarray(x, np.float32).astype(BF16)


def f64(x):
    return np.asarray(x).astype(np.float64)


E2M1 = np.array([0.0, 0.5, 1.0, 1.5, 2.0, 3.0, 4.0, 6.0, -0.0, -0.5, -1.0, -1.5, -2.0, -3.0, -4.0, -6.0])


def pack_weight(w, fmt):
    k, n = w.shape
    w = f64(bf(w)).reshape(k // 32, 32, n)
    amax = np.abs(w).max(1)
    if fmt == "e4m3":
        byte = np.frexp(amax)[1] - 1 + 127 - 7
    else:
        mant, ex = np.frexp(amax / 6.0)
        byte = np.where(mant > 0.5, ex, ex - 1) + 127
    byte = np.clip(np.where(amax > 0, byte, 1), 1, 254)
    scaled = (w * np.exp2(127.0 - byte)[:, None, :]).reshape(k, n).astype(np.float32)
    by_word = np.ascontiguousarray(scaled.reshape(k // 512, 128, 4, n).transpose(0, 1, 3, 2))
    if fmt == "e4m3":
        words = by_word.astype(ml_dtypes.float8_e4m3fn).view(np.uint8)
    else:
        c = by_word.astype(ml_dtypes.float4_e2m1fn).view(np.uint8) & 0xF
        words = c[..., 0::2] | (c[..., 1::2] << 4)
    return np.ascontiguousarray(words), np.ascontiguousarray(byte.astype(np.uint8).reshape(k // 512, 16, n))


def unpack_weight(words, scales, fmt):
    g, p, n, _ = words.shape
    if fmt == "e4m3":
        vals = np.ascontiguousarray(words).view(ml_dtypes.float8_e4m3fn).astype(np.float64)
    else:
        nib = np.empty((g, p, n, 4), np.uint8)
        nib[..., 0::2] = words & 0xF
        nib[..., 1::2] = words >> 4
        vals = E2M1[nib]
    vals = vals * np.repeat(np.exp2(scales.astype(np.float64) - 127.0), 8, axis=1)[..., None]
    return vals.transpose(0, 1, 3, 2).reshape(g * 512, n)


B, N, DIM, HEADS, DIM_HEAD = 2, 512, 1024, 16, 64
INNER = HEADS * DIM_HEAD
FMT = "e4m3"


def setup_inputs():
    s = mx_kscale(DIM)
    x = bf(np.random.standard_normal((B, N, DIM)) * s)
    w = np.random.standard_normal((3 * INNER, DIM)) / np.sqrt(DIM) / s[None, :]
    words, scales = pack_weight(np.ascontiguousarray(w.T), FMT)
    return {"x": x, "W_words": words, "W_scales": scales}


def reference(x, W_words, W_scales):
    b, n, _ = x.shape
    qkv = mxq(f64(x), 2, "e4m3") @ unpack_weight(W_words, W_scales, FMT)
    q, k, v = np.split(qkv, 3, axis=-1)

    def to_heads(t):
        return t.reshape(b, n, HEADS, DIM_HEAD).transpose(0, 2, 1, 3)

    return to_heads(q), to_heads(k), to_heads(v)

@@ -1,0 +1,132 @@
+from contextlib import ExitStack
+
+import concourse.mybir as mybir
+from concourse.masks import make_identity
+
+F32 = mybir.dt.float32
+BF16 = mybir.dt.bfloat16
+I32 = mybir.dt.int32
+U32 = mybir.dt.uint32
+U8 = mybir.dt.uint8
+FP8X4 = mybir.dt.float8_e4m3fn_x4
+
+P = 128
+PACK = 4
+K_PASS = P * PACK
+N_TILE = 512
+PAIR = 2
+
+FLOPS = 2 * 1024 * 1024 * 3072
+
+
+def tile_get_qkv_kernel(tc, x, W_words, W_scales, out_0, out_1, out_2):
+    nc = tc.nc
+    batches, tokens, dim = x.shape
+    heads, dim_head = out_0.shape[1], out_0.shape[3]
+    columns = W_scales.shape[2]
+    passes = dim // K_PASS
+    token_tiles = batches * tokens // P
+    column_tiles = columns // N_TILE
+    tile_heads = N_TILE // dim_head
+    store_heads = 4
+    words_per_pass = K_PASS // PAIR
+    parts = (out_0, out_1, out_2)
+
+    with ExitStack() as ctx:
+        ctx.enter_context(tc.manual_schedule())
+        keep = ctx.enter_context(tc.tile_pool(name="keep", bufs=1))
+        psum = ctx.enter_context(tc.psum_pool(name="psum", bufs=8))
+
+        def leave_psum(t, out, in_):
+            if t % 2 == 0:
+                nc.vector.tensor_copy(out=out, in_=in_)
+            else:
+                nc.scalar.copy(out=out, in_=in_)
+
+        x_rows = []
+        for first in range(0, token_tiles, 2):
+            rows = keep.tile([P, 2, dim], BF16, name="x_rows%d" % first)
+            for b in range(batches):
+                nc.sync.dma_start(
+                    out=rows[b:P:batches, :, :],
+                    in_=x[b].rearrange("(i t) d -> i t d", t=token_tiles)[:, first : first + 2, :],
+                )
+            x_rows.append(rows)
+
+        w_planes = keep.tile([P, passes, columns], U8, align_bytes=64)
+        nc.vector.memset(w_planes[:].bitcast(I32), 0)
+        for g in range(passes):
+            for q in range(8):
+                nc.sync.dma_start(
+                    out=w_planes[32 * (q // 4) + q % 4 : P : 64, g, :].bitcast(I32),
+                    in_=W_scales[g, q:16:8, :].bitcast(I32),
+                )
+
+        w_words = []
+        for c in range(column_tiles):
+            words = keep.tile([P, passes, N_TILE], U32, align_bytes=64, name="w_words%d" % c)
+            nc.sync.dma_start(
+                out=words[:].bitcast(I32),
+                in_=W_words.rearrange("g p n j -> p g (n j)")[
+                    :, :, PACK * N_TILE * c : PACK * N_TILE * (c + 1)
+                ].bitcast(I32),
+            )
+            w_words.append(words)
+
+        identity = keep.tile([P, P], F32)
+        make_identity(nc, identity[:])
+        x_codes = keep.tile([P, token_tiles, passes * P], U32, align_bytes=64)
+        x_scales = keep.tile([P, token_tiles, passes * P], U8, align_bytes=64)
+
+        def quantise(t, grouped):
+            nc.vector.quantize_mx(
+                out=x_codes[:, t, :].bitcast(FP8X4),
+                scales=x_scales[:, t, :],
+                in_=grouped[:].rearrange("p g m j -> p (g m j)"),
+            )
+
+        grouped_tiles = []
+        for t in range(token_tiles):
+            row_words = x_rows[t // 2][:, t % 2, :].bitcast(F32)
+            halves = psum.tile([P, passes, PAIR, P], F32, tag="bank")
+            for g in range(passes):
+                for u in range(PAIR):
+                    nc.tensor.transpose(
+                        halves[:, g, u, :],
+                        row_words[:, words_per_pass * g + u : words_per_pass * (g + 1) : PAIR],
+                        identity[:],
+                    )
+            grouped = keep.tile([P, passes, P, PACK], BF16, align_bytes=64, name="grouped%d" % t)
+            leave_psum(t, grouped[:].bitcast(F32), halves[:].rearrange("p g u m -> p g m u"))
+            grouped_tiles.append(grouped)
+            if t >= 1:
+                quantise(t - 1, grouped_tiles[t - 1])
+        quantise(token_tiles - 1, grouped_tiles[token_tiles - 1])
+
+        for c in range(column_tiles):
+            part = parts[c * N_TILE // (heads * dim_head)]
+            first_head = c * tile_heads % heads
+            result = keep.tile([P, tile_heads, token_tiles, dim_head], F32, name="result%d" % c)
+            for t in range(token_tiles):
+                acc = psum.tile([P, N_TILE], F32, tag="bank")
+                for g in range(passes):
+                    nc.tensor.matmul_mx(
+                        out=acc[:],
+                        lhsT=x_codes[:, t, P * g : P * (g + 1)].bitcast(FP8X4),
+                        lhsT_scale=x_scales[:, t, P * g : P * (g + 1)],
+                        rhs=w_words[c][:, g, :].bitcast(FP8X4),
+                        rhs_scale=w_planes[:, g, N_TILE * c : N_TILE * (c + 1)],
+                        start=(g == 0),
+                        stop=(g == passes - 1),
+                    )
+                leave_psum(t, result[:, :, t, :], acc[:].rearrange("p (h e) -> p h e", e=dim_head))
+            for b in range(batches):
+                for h in range(0, tile_heads, store_heads):
+                    nc.sync.dma_start(
+                        out=part[b, first_head + h : first_head + h + store_heads].rearrange(
+                            "h (i t) e -> i h (t e)", t=token_tiles
+                        ),
+                        in_=result[b:P:batches, h : h + store_heads, :, :].rearrange(
+                            "p h t e -> p h (t e)"
+                        ),
+                    )

@@ -55,12 +55,11 @@ def tile_get_qkv_kernel(tc, x, W_words, W_scales, out_0, out_1, out_2):
 
         w_planes = keep.tile([P, passes, columns], U8, align_bytes=64)
         nc.vector.memset(w_planes[:].bitcast(I32), 0)
-        for g in range(passes):
-            for q in range(8):
-                nc.sync.dma_start(
-                    out=w_planes[32 * (q // 4) + q % 4 : P : 64, g, :].bitcast(I32),
-                    in_=W_scales[g, q:16:8, :].bitcast(I32),
-                )
+        for r in range(4):
+            nc.sync.dma_start(
+                out=w_planes[r:P:32, :, :].bitcast(I32),
+                in_=W_scales[:, r:16:4, :].rearrange("g q n -> q g n").bitcast(I32),
+            )
 
         w_words = []
         for c in range(column_tiles):

@@ -13,7 +13,8 @@ FP8X4 = mybir.dt.float8_e4m3fn_x4
 P = 128
 PACK = 4
 K_PASS = P * PACK
-N_TILE = 512
+N_TILE = 256
+LOAD_TILES = 2
 PAIR = 2
 
 FLOPS = 2 * 1024 * 1024 * 3072
@@ -28,7 +29,6 @@ def tile_get_qkv_kernel(tc, x, W_words, W_scales, out_0, out_1, out_2):
     token_tiles = batches * tokens // P
     column_tiles = columns // N_TILE
     tile_heads = N_TILE // dim_head
-    store_heads = 4
     words_per_pass = K_PASS // PAIR
     parts = (out_0, out_1, out_2)
 
@@ -61,13 +61,14 @@ def tile_get_qkv_kernel(tc, x, W_words, W_scales, out_0, out_1, out_2):
                 in_=W_scales[:, r:16:4, :].rearrange("g q n -> q g n").bitcast(I32),
             )
 
+        load_columns = LOAD_TILES * N_TILE
         w_words = []
-        for c in range(column_tiles):
-            words = keep.tile([P, passes, N_TILE], U32, align_bytes=64, name="w_words%d" % c)
+        for first in range(0, columns, load_columns):
+            words = keep.tile([P, passes, load_columns], U32, align_bytes=64, name="w_words%d" % first)
             nc.sync.dma_start(
                 out=words[:].bitcast(I32),
                 in_=W_words.rearrange("g p n j -> p g (n j)")[
-                    :, :, PACK * N_TILE * c : PACK * N_TILE * (c + 1)
+                    :, :, PACK * first : PACK * (first + load_columns)
                 ].bitcast(I32),
             )
             w_words.append(words)
@@ -113,19 +114,18 @@ def tile_get_qkv_kernel(tc, x, W_words, W_scales, out_0, out_1, out_2):
                         out=acc[:],
                         lhsT=x_codes[:, t, P * g : P * (g + 1)].bitcast(FP8X4),
                         lhsT_scale=x_scales[:, t, P * g : P * (g + 1)],
-                        rhs=w_words[c][:, g, :].bitcast(FP8X4),
+                        rhs=w_words[c // LOAD_TILES][
+                            :, g, N_TILE * (c % LOAD_TILES) : N_TILE * (c % LOAD_TILES + 1)
+                        ].bitcast(FP8X4),
                         rhs_scale=w_planes[:, g, N_TILE * c : N_TILE * (c + 1)],
                         start=(g == 0),
                         stop=(g == passes - 1),
                     )
                 leave_psum(t, result[:, :, t, :], acc[:].rearrange("p (h e) -> p h e", e=dim_head))
             for b in range(batches):
-                for h in range(0, tile_heads, store_heads):
-                    nc.sync.dma_start(
-                        out=part[b, first_head + h : first_head + h + store_heads].rearrange(
-                            "h (i t) e -> i h (t e)", t=token_tiles
-                        ),
-                        in_=result[b:P:batches, h : h + store_heads, :, :].rearrange(
-                            "p h t e -> p h (t e)"
-                        ),
-                    )
+                nc.sync.dma_start(
+                    out=part[b, first_head : first_head + tile_heads].rearrange(
+                        "h (i t) e -> i h (t e)", t=token_tiles
+                    ),
+                    in_=result[b:P:batches, :, :, :].rearrange("p h t e -> p h (t e)"),
+                )

@@ -14,6 +14,7 @@ P = 128
 PACK = 4
 K_PASS = P * PACK
 N_TILE = 256
+LAST_TILE = 128
 LOAD_TILES = 2
 PAIR = 2
 
@@ -28,7 +29,6 @@ def tile_get_qkv_kernel(tc, x, W_words, W_scales, out_0, out_1, out_2):
     passes = dim // K_PASS
     token_tiles = batches * tokens // P
     column_tiles = columns // N_TILE
-    tile_heads = N_TILE // dim_head
     words_per_pass = K_PASS // PAIR
     parts = (out_0, out_1, out_2)
 
@@ -103,21 +103,23 @@ def tile_get_qkv_kernel(tc, x, W_words, W_scales, out_0, out_1, out_2):
                 quantise(t - 1, grouped_tiles[t - 1])
         quantise(token_tiles - 1, grouped_tiles[token_tiles - 1])
 
-        for c in range(column_tiles):
-            part = parts[c * N_TILE // (heads * dim_head)]
-            first_head = c * tile_heads % heads
+        widths = [N_TILE] * (column_tiles - 1) + [LAST_TILE] * (N_TILE // LAST_TILE)
+        for c, width in enumerate(widths):
+            first = sum(widths[:c])
+            part = parts[first // (heads * dim_head)]
+            first_head = first // dim_head % heads
+            tile_heads = width // dim_head
+            in_load = first % load_columns
             result = keep.tile([P, tile_heads, token_tiles, dim_head], F32, name="result%d" % c)
             for t in range(token_tiles):
-                acc = psum.tile([P, N_TILE], F32, tag="bank")
+                acc = psum.tile([P, width], F32, tag="bank")
                 for g in range(passes):
                     nc.tensor.matmul_mx(
                         out=acc[:],
                         lhsT=x_codes[:, t, P * g : P * (g + 1)].bitcast(FP8X4),
                         lhsT_scale=x_scales[:, t, P * g : P * (g + 1)],
-                        rhs=w_words[c // LOAD_TILES][
-                            :, g, N_TILE * (c % LOAD_TILES) : N_TILE * (c % LOAD_TILES + 1)
-                        ].bitcast(FP8X4),
-                        rhs_scale=w_planes[:, g, N_TILE * c : N_TILE * (c + 1)],
+                        rhs=w_words[first // load_columns][:, g, in_load : in_load + width].bitcast(FP8X4),
+                        rhs_scale=w_planes[:, g, first : first + width],
                         start=(g == 0),
                         stop=(g == passes - 1),
                     )

@@ -53,17 +53,23 @@ def tile_get_qkv_kernel(tc, x, W_words, W_scales, out_0, out_1, out_2):
                 )
             x_rows.append(rows)
 
+        load_columns = LOAD_TILES * N_TILE
         w_planes = keep.tile([P, passes, columns], U8, align_bytes=64)
         nc.vector.memset(w_planes[:].bitcast(I32), 0)
-        for r in range(4):
-            nc.sync.dma_start(
-                out=w_planes[r:P:32, :, :].bitcast(I32),
-                in_=W_scales[:, r:16:4, :].rearrange("g q n -> q g n").bitcast(I32),
-            )
 
-        load_columns = LOAD_TILES * N_TILE
+        def load_scales(first, last):
+            for r in range(4):
+                nc.sync.dma_start(
+                    out=w_planes[r:P:32, :, first:last].bitcast(I32),
+                    in_=W_scales[:, r:16:4, first:last].rearrange("g q n -> q g n").bitcast(I32),
+                )
+
         w_words = []
         for first in range(0, columns, load_columns):
+            if first == 0:
+                load_scales(0, load_columns)
+            elif first == load_columns:
+                load_scales(load_columns, columns)
             words = keep.tile([P, passes, load_columns], U32, align_bytes=64, name="w_words%d" % first)
             nc.sync.dma_start(
                 out=words[:].bitcast(I32),

@@ -43,14 +43,11 @@ def tile_get_qkv_kernel(tc, x, W_words, W_scales, out_0, out_1, out_2):
             else:
                 nc.scalar.copy(out=out, in_=in_)
 
+        x_groups = x.rearrange("b (i t) d -> (b i) t d", t=token_tiles)
         x_rows = []
         for first in range(0, token_tiles, 2):
             rows = keep.tile([P, 2, dim], BF16, name="x_rows%d" % first)
-            for b in range(batches):
-                nc.sync.dma_start(
-                    out=rows[b:P:batches, :, :],
-                    in_=x[b].rearrange("(i t) d -> i t d", t=token_tiles)[:, first : first + 2, :],
-                )
+            nc.sync.dma_start(out=rows[:], in_=x_groups[:, first : first + 2, :])
             x_rows.append(rows)
 
         load_columns = LOAD_TILES * N_TILE
@@ -81,6 +78,11 @@ def tile_get_qkv_kernel(tc, x, W_words, W_scales, out_0, out_1, out_2):
 
         identity = keep.tile([P, P], F32)
         make_identity(nc, identity[:])
+        shuffle = keep.tile([P, P], F32)
+        nc.vector.tensor_copy(
+            out=shuffle[:].rearrange("p (i b) -> p b i", b=batches),
+            in_=identity[:].rearrange("p (b i) -> p b i", b=batches),
+        )
         x_codes = keep.tile([P, token_tiles, passes * P], U32, align_bytes=64)
         x_scales = keep.tile([P, token_tiles, passes * P], U8, align_bytes=64)
 
@@ -100,7 +102,7 @@ def tile_get_qkv_kernel(tc, x, W_words, W_scales, out_0, out_1, out_2):
                     nc.tensor.transpose(
                         halves[:, g, u, :],
                         row_words[:, words_per_pass * g + u : words_per_pass * (g + 1) : PAIR],
-                        identity[:],
+                        shuffle[:],
                     )
             grouped = keep.tile([P, passes, P, PACK], BF16, align_bytes=64, name="grouped%d" % t)
             leave_psum(t, grouped[:].bitcast(F32), halves[:].rearrange("p g u m -> p g m u"))

@@ -15,7 +15,8 @@ PACK = 4
 K_PASS = P * PACK
 N_TILE = 256
 LAST_TILE = 128
-LOAD_TILES = 2
+LOADS = (256, 256, 512, 2048)
+EARLY_SCALES = 512
 PAIR = 2
 
 FLOPS = 2 * 1024 * 1024 * 3072
@@ -50,7 +51,6 @@ def tile_get_qkv_kernel(tc, x, W_words, W_scales, out_0, out_1, out_2):
             nc.sync.dma_start(out=rows[:], in_=x_groups[:, first : first + 2, :])
             x_rows.append(rows)
 
-        load_columns = LOAD_TILES * N_TILE
         w_planes = keep.tile([P, passes, columns], U8, align_bytes=64)
         nc.vector.memset(w_planes[:].bitcast(I32), 0)
 
@@ -61,12 +61,13 @@ def tile_get_qkv_kernel(tc, x, W_words, W_scales, out_0, out_1, out_2):
                     in_=W_scales[:, r:16:4, first:last].rearrange("g q n -> q g n").bitcast(I32),
                 )
 
-        w_words = []
-        for first in range(0, columns, load_columns):
+        w_words = {}
+        for number, load_columns in enumerate(LOADS):
+            first = sum(LOADS[:number])
             if first == 0:
-                load_scales(0, load_columns)
-            elif first == load_columns:
-                load_scales(load_columns, columns)
+                load_scales(0, EARLY_SCALES)
+            elif first == EARLY_SCALES:
+                load_scales(EARLY_SCALES, columns)
             words = keep.tile([P, passes, load_columns], U32, align_bytes=64, name="w_words%d" % first)
             nc.sync.dma_start(
                 out=words[:].bitcast(I32),
@@ -74,7 +75,7 @@ def tile_get_qkv_kernel(tc, x, W_words, W_scales, out_0, out_1, out_2):
                     :, :, PACK * first : PACK * (first + load_columns)
                 ].bitcast(I32),
             )
-            w_words.append(words)
+            w_words[first] = words
 
         identity = keep.tile([P, P], F32)
         make_identity(nc, identity[:])
@@ -117,7 +118,8 @@ def tile_get_qkv_kernel(tc, x, W_words, W_scales, out_0, out_1, out_2):
             part = parts[first // (heads * dim_head)]
             first_head = first // dim_head % heads
             tile_heads = width // dim_head
-            in_load = first % load_columns
+            load_first = max([start for start in w_words if start <= first])
+            in_load = first - load_first
             result = keep.tile([P, tile_heads, token_tiles, dim_head], F32, name="result%d" % c)
             for t in range(token_tiles):
                 acc = psum.tile([P, width], F32, tag="bank")
@@ -126,7 +128,7 @@ def tile_get_qkv_kernel(tc, x, W_words, W_scales, out_0, out_1, out_2):
                         out=acc[:],
                         lhsT=x_codes[:, t, P * g : P * (g + 1)].bitcast(FP8X4),
                         lhsT_scale=x_scales[:, t, P * g : P * (g + 1)],
-                        rhs=w_words[first // load_columns][:, g, in_load : in_load + width].bitcast(FP8X4),
+                        rhs=w_words[load_first][:, g, in_load : in_load + width].bitcast(FP8X4),
                         rhs_scale=w_planes[:, g, first : first + width],
                         start=(g == 0),
                         stop=(g == passes - 1),

@@ -66,7 +66,7 @@ def tile_get_qkv_kernel(tc, x, W_words, W_scales, out_0, out_1, out_2):
             first = sum(LOADS[:number])
             if first == 0:
                 load_scales(0, EARLY_SCALES)
-            elif first == EARLY_SCALES:
+            elif number == len(LOADS) - 1:
                 load_scales(EARLY_SCALES, columns)
             words = keep.tile([P, passes, load_columns], U32, align_bytes=64, name="w_words%d" % first)
             nc.sync.dma_start(

@@ -15,7 +15,7 @@ PACK = 4
 K_PASS = P * PACK
 N_TILE = 256
 LAST_TILE = 128
-LOADS = (256, 256, 512, 2048)
+LOADS = (256, 768, 2048)
 EARLY_SCALES = 512
 PAIR = 2
 

from contextlib import ExitStack

import concourse.mybir as mybir
from concourse.masks import make_identity

F32 = mybir.dt.float32
BF16 = mybir.dt.bfloat16
I32 = mybir.dt.int32
U32 = mybir.dt.uint32
U8 = mybir.dt.uint8
FP8X4 = mybir.dt.float8_e4m3fn_x4

P = 128
PACK = 4
K_PASS = P * PACK
N_TILE = 256
LAST_TILE = 128
LOADS = (256, 768, 2048)
EARLY_SCALES = 512
PAIR = 2

FLOPS = 2 * 1024 * 1024 * 3072


def tile_get_qkv_kernel(tc, x, W_words, W_scales, out_0, out_1, out_2):
    nc = tc.nc
    batches, tokens, dim = x.shape
    heads, dim_head = out_0.shape[1], out_0.shape[3]
    columns = W_scales.shape[2]
    passes = dim // K_PASS
    token_tiles = batches * tokens // P
    column_tiles = columns // N_TILE
    words_per_pass = K_PASS // PAIR
    parts = (out_0, out_1, out_2)

    with ExitStack() as ctx:
        ctx.enter_context(tc.manual_schedule())
        keep = ctx.enter_context(tc.tile_pool(name="keep", bufs=1))
        psum = ctx.enter_context(tc.psum_pool(name="psum", bufs=8))

        def leave_psum(t, out, in_):
            if t % 2 == 0:
                nc.vector.tensor_copy(out=out, in_=in_)
            else:
                nc.scalar.copy(out=out, in_=in_)

        x_groups = x.rearrange("b (i t) d -> (b i) t d", t=token_tiles)
        x_rows = []
        for first in range(0, token_tiles, 2):
            rows = keep.tile([P, 2, dim], BF16, name="x_rows%d" % first)
            nc.sync.dma_start(out=rows[:], in_=x_groups[:, first : first + 2, :])
            x_rows.append(rows)

        w_planes = keep.tile([P, passes, columns], U8, align_bytes=64)
        nc.vector.memset(w_planes[:].bitcast(I32), 0)

        def load_scales(first, last):
            for r in range(4):
                nc.sync.dma_start(
                    out=w_planes[r:P:32, :, first:last].bitcast(I32),
                    in_=W_scales[:, r:16:4, first:last].rearrange("g q n -> q g n").bitcast(I32),
                )

        w_words = {}
        for number, load_columns in enumerate(LOADS):
            first = sum(LOADS[:number])
            if first == 0:
                load_scales(0, EARLY_SCALES)
            elif number == len(LOADS) - 1:
                load_scales(EARLY_SCALES, columns)
            words = keep.tile([P, passes, load_columns], U32, align_bytes=64, name="w_words%d" % first)
            nc.sync.dma_start(
                out=words[:].bitcast(I32),
                in_=W_words.rearrange("g p n j -> p g (n j)")[
                    :, :, PACK * first : PACK * (first + load_columns)
                ].bitcast(I32),
            )
            w_words[first] = words

        identity = keep.tile([P, P], F32)
        make_identity(nc, identity[:])
        shuffle = keep.tile([P, P], F32)
        nc.vector.tensor_copy(
            out=shuffle[:].rearrange("p (i b) -> p b i", b=batches),
            in_=identity[:].rearrange("p (b i) -> p b i", b=batches),
        )
        x_codes = keep.tile([P, token_tiles, passes * P], U32, align_bytes=64)
        x_scales = keep.tile([P, token_tiles, passes * P], U8, align_bytes=64)

        def quantise(t, grouped):
            nc.vector.quantize_mx(
                out=x_codes[:, t, :].bitcast(FP8X4),
                scales=x_scales[:, t, :],
                in_=grouped[:].rearrange("p g m j -> p (g m j)"),
            )

        grouped_tiles = []
        for t in range(token_tiles):
            row_words = x_rows[t // 2][:, t % 2, :].bitcast(F32)
            halves = psum.tile([P, passes, PAIR, P], F32, tag="bank")
            for g in range(passes):
                for u in range(PAIR):
                    nc.tensor.transpose(
                        halves[:, g, u, :],
                        row_words[:, words_per_pass * g + u : words_per_pass * (g + 1) : PAIR],
                        shuffle[:],
                    )
            grouped = keep.tile([P, passes, P, PACK], BF16, align_bytes=64, name="grouped%d" % t)
            leave_psum(t, grouped[:].bitcast(F32), halves[:].rearrange("p g u m -> p g m u"))
            grouped_tiles.append(grouped)
            if t >= 1:
                quantise(t - 1, grouped_tiles[t - 1])
        quantise(token_tiles - 1, grouped_tiles[token_tiles - 1])

        widths = [N_TILE] * (column_tiles - 1) + [LAST_TILE] * (N_TILE // LAST_TILE)
        for c, width in enumerate(widths):
            first = sum(widths[:c])
            part = parts[first // (heads * dim_head)]
            first_head = first // dim_head % heads
            tile_heads = width // dim_head
            load_first = max([start for start in w_words if start <= first])
            in_load = first - load_first
            result = keep.tile([P, tile_heads, token_tiles, dim_head], F32, name="result%d" % c)
            for t in range(token_tiles):
                acc = psum.tile([P, width], F32, tag="bank")
                for g in range(passes):
                    nc.tensor.matmul_mx(
                        out=acc[:],
                        lhsT=x_codes[:, t, P * g : P * (g + 1)].bitcast(FP8X4),
                        lhsT_scale=x_scales[:, t, P * g : P * (g + 1)],
                        rhs=w_words[load_first][:, g, in_load : in_load + width].bitcast(FP8X4),
                        rhs_scale=w_planes[:, g, first : first + width],
                        start=(g == 0),
                        stop=(g == passes - 1),
                    )
                leave_psum(t, result[:, :, t, :], acc[:].rearrange("p (h e) -> p h e", e=dim_head))
            for b in range(batches):
                nc.sync.dma_start(
                    out=part[b, first_head : first_head + tile_heads].rearrange(
                        "h (i t) e -> i h (t e)", t=token_tiles
                    ),
                    in_=result[b:P:batches, :, :, :].rearrange("p h t e -> p h (t e)"),
                )
